import numpy as np
import ml_dtypes


def mxq(x, axis, fmt="e4m3"):
    dtype, down = {"e4m3": (ml_dtypes.float8_e4m3fn, 7), "e5m2": (ml_dtypes.float8_e5m2, 14)}[fmt]
    v = np.moveaxis(np.asarray(x, np.float32).astype(ml_dtypes.bfloat16).astype(np.float64), axis, -1)
    blocks = v.reshape(v.shape[:-1] + (-1, 32))
    amax = np.abs(blocks).max(-1, keepdims=True)
    byte = np.maximum(np.where(amax > 0, np.frexp(amax)[1] - 1 + 127, 0) - down, 1)
    scale = np.exp2(byte - 127.0)
    codes = (blocks / scale).astype(np.float32).astype(dtype).astype(np.float64)
    return np.moveaxis((codes * scale).reshape(v.shape), -1, axis)


WIDE = False


def mx_kscale(k):
    if not WIDE:
        return np.ones(k)
    levels = np.array([10, -10, 5, -5, 0])
    a = np.random.permutation(np.resize(levels, k // 512 * 4)).reshape(k // 512, 4)
    idx = np.arange(k)
    return np.exp2(a[idx // 512, idx % 128 // 32])


BF16 = ml_dtypes.bfloat16


def bf(x):
    return np.asarray(x, np.float32).astype(BF16)


def f64(x):
    return np.asarray(x).astype(np.float64)


E2M1 = np.array([0.0, 0.5, 1.0, 1.5, 2.0, 3.0, 4.0, 6.0, -0.0, -0.5, -1.0, -1.5, -2.0, -3.0, -4.0, -6.0])


def pack_weight(w, fmt):
    k, n = w.shape
    w = f64(bf(w)).reshape(k // 32, 32, n)
    amax = np.abs(w).max(1)
    if fmt == "e4m3":
        byte = np.frexp(amax)[1] - 1 + 127 - 7
    else:
        mant, ex = np.frexp(amax / 6.0)
        byte = np.where(mant > 0.5, ex, ex - 1) + 127
    byte = np.clip(np.where(amax > 0, byte, 1), 1, 254)
    scaled = (w * np.exp2(127.0 - byte)[:, None, :]).reshape(k, n).astype(np.float32)
    by_word = np.ascontiguousarray(scaled.reshape(k // 512, 128, 4, n).transpose(0, 1, 3, 2))
    if fmt == "e4m3":
        words = by_word.astype(ml_dtypes.float8_e4m3fn).view(np.uint8)
    else:
        c = by_word.astype(ml_dtypes.float4_e2m1fn).view(np.uint8) & 0xF
        words = c[..., 0::2] | (c[..., 1::2] << 4)
    return np.ascontiguousarray(words), np.ascontiguousarray(byte.astype(np.uint8).reshape(k // 512, 16, n))


def unpack_weight(words, scales, fmt):
    g, p, n, _ = words.shape
    if fmt == "e4m3":
        vals = np.ascontiguousarray(words).view(ml_dtypes.float8_e4m3fn).astype(np.float64)
    else:
        nib = np.empty((g, p, n, 4), np.uint8)
        nib[..., 0::2] = words & 0xF
        nib[..., 1::2] = words >> 4
        vals = E2M1[nib]
    vals = vals * np.repeat(np.exp2(scales.astype(np.float64) - 127.0), 8, axis=1)[..., None]
    return vals.transpose(0, 1, 3, 2).reshape(g * 512, n)


B, I, HS, G = 512, 1024, 512, 2
H = HS * G
MXK = 16 * 32
HH_MX = H % MXK == 0


def sigmoid(v):
    return 1.0 / (1.0 + np.exp(-v))


def setup_inputs():
    s = mx_kscale(I)
    t = mx_kscale(H) if HH_MX else np.ones(H)
    inp = bf(np.random.standard_normal((B, I)) * s)
    h0 = bf(np.random.standard_normal((B, H)) * t)
    c0 = bf(np.random.standard_normal((B, H)))
    ih_words, ih_scales = pack_weight(np.random.standard_normal((I, 4 * H)) * 0.7 / np.sqrt(I) / s[:, None], "e4m3")
    hh_words, hh_scales = pack_weight(np.random.standard_normal((H, 4 * H)) * 0.7 / np.sqrt(H) / t[:, None], "e4m3")
    return {"input": inp,
            "h0": h0,
            "c0": c0,
            "weight_ih_words": ih_words,
            "weight_ih_scales": ih_scales,
            "weight_hh_words": hh_words,
            "weight_hh_scales": hh_scales,
            "bias_ih": bf(np.random.standard_normal(4 * H) * 0.3),
            "bias_hh": bf(np.random.standard_normal(4 * H) * 0.3)}


def reference(input, h0, c0, weight_ih_words, weight_ih_scales, weight_hh_words, weight_hh_scales, bias_ih, bias_hh):
    pi = mxq(f64(input), 1, "e4m3") @ unpack_weight(weight_ih_words, weight_ih_scales, "e4m3")
    if HH_MX:
        ph = mxq(f64(h0), 1, "e4m3") @ unpack_weight(weight_hh_words, weight_hh_scales, "e4m3")
    else:
        ph = f64(h0) @ unpack_weight(weight_hh_words, weight_hh_scales, "e4m3")
    gates = pi + f64(bias_ih) + ph + f64(bias_hh)
    c_in = f64(c0)
    h_parts, c_parts = [], []
    st = 0
    for _ in range(G):
        blk = gates[:, st * 4: st * 4 + 4 * HS]
        g, i, f, o = np.split(blk, 4, axis=-1)
        c1 = np.tanh(g) * sigmoid(i) + c_in[:, st: st + HS] * sigmoid(f)
        h_parts.append(np.tanh(c1) * sigmoid(o))
        c_parts.append(c1)
        st += HS
    return np.concatenate(h_parts, axis=-1), np.concatenate(c_parts, axis=-1)

@@ -1,0 +1,215 @@
+from contextlib import ExitStack
+
+import concourse.mybir as mybir
+from concourse.masks import make_identity
+
+F32 = mybir.dt.float32
+BF16 = mybir.dt.bfloat16
+I32 = mybir.dt.int32
+U32 = mybir.dt.uint32
+U8 = mybir.dt.uint8
+FP8X4 = mybir.dt.float8_e4m3fn_x4
+ADD = mybir.AluOpType.add
+MULT = mybir.AluOpType.mult
+TANH = mybir.ActivationFunctionType.Tanh
+SIGMOID = mybir.ActivationFunctionType.Sigmoid
+
+P = 128
+BATCH = 512
+M_TILES = BATCH // P
+WIDTH = 1024
+K_PASS = 4 * P
+HALVES = WIDTH // K_PASS
+PASSES = 2 * HALVES
+HS = 512
+GATES = 4
+GROUPS = 2
+CHUNKS = GROUPS * GATES
+GATE_COLS = CHUNKS * HS
+STEPS = CHUNKS * M_TILES
+LAG = 2
+
+FLOPS = 2 * BATCH * (2 * WIDTH) * GATE_COLS
+
+
+def tile_symlstmcell_kernel(
+    tc,
+    x_in,
+    h0,
+    c0,
+    w_ih_words,
+    w_ih_scales,
+    w_hh_words,
+    w_hh_scales,
+    bias_ih,
+    bias_hh,
+    h1_out,
+    c1_out,
+):
+    nc = tc.nc
+    sources = (x_in, h0)
+    words = (w_ih_words, w_hh_words)
+    scales = (w_ih_scales, w_hh_scales)
+
+    with ExitStack() as ctx:
+        keep = ctx.enter_context(tc.tile_pool(name="keep", bufs=1))
+        work = ctx.enter_context(tc.tile_pool(name="work", bufs=M_TILES))
+        psum = ctx.enter_context(tc.psum_pool(name="psum", bufs=8))
+
+        x_raw = keep.tile([P, 2, M_TILES, WIDTH], BF16)
+        x_grouped = keep.tile([P, M_TILES, PASSES, 4 * P], BF16, align_bytes=64)
+        x_codes = keep.tile([P, M_TILES, PASSES, P], U32, align_bytes=64)
+        x_scales = keep.tile([P, M_TILES, PASSES, P], U8, align_bytes=64)
+        w_codes = keep.tile([P, PASSES, GATE_COLS], U32, align_bytes=64)
+        w_planes = keep.tile([P, GATE_COLS], U8, align_bytes=64)
+        c0_sb = keep.tile([P, M_TILES, WIDTH], BF16)
+        bias_rows = keep.tile([P, HS], BF16)
+        bias_pick = keep.tile([P, CHUNKS], BF16)
+        bias_sb = keep.tile([P, CHUNKS, HS], F32)
+        ident = keep.tile([P, P], F32)
+        warm = keep.tile([P, 1], F32)
+
+        nc.vector.memset(w_planes[:].bitcast(I32), 0)
+        nc.vector.memset(bias_rows[:], 0.0)
+        nc.vector.memset(warm[:], 0.0)
+        make_identity(nc, ident[:])
+        nc.scalar.activation(out=warm[:], in_=warm[:], func=SIGMOID)
+
+        def load_weight_scales(s):
+            for quad in range(4):
+                first = 32 * quad + 4 * HALVES * s
+                nc.sync.dma_start(
+                    out=w_planes[first : first + 4 * HALVES, :].bitcast(I32),
+                    in_=scales[s][:, 4 * quad : 4 * quad + 4, :].bitcast(I32),
+                )
+
+        def load_x(s, half):
+            rows = sources[s][2 * P * half : 2 * P * (half + 1), :]
+            nc.scalar.dma_start(
+                out=x_raw[:, s, 2 * half : 2 * half + 2, :],
+                in_=rows.rearrange("(m p) k -> p m k", p=P),
+            )
+
+        def load_weight_chunk(s, n):
+            all_words = words[s].rearrange("g p n t -> p g (n t)").bitcast(I32)
+            nc.sync.dma_start(
+                out=w_codes[:, HALVES * s : HALVES * (s + 1), HS * n : HS * (n + 1)].bitcast(I32),
+                in_=all_words[:, :, HS * n : HS * (n + 1)],
+            )
+
+        load_weight_scales(0)
+        for s in range(2):
+            for half in range(2):
+                load_x(s, half)
+        load_weight_scales(1)
+        nc.gpsimd.dma_start(out=bias_rows[0:CHUNKS, :], in_=bias_ih.rearrange("(n c) -> n c", c=HS))
+        nc.gpsimd.dma_start(
+            out=bias_rows[CHUNKS : 2 * CHUNKS, :], in_=bias_hh.rearrange("(n c) -> n c", c=HS)
+        )
+        for n in range(CHUNKS):
+            for s in range(2):
+                load_weight_chunk(s, n)
+            if n == 1:
+                nc.sync.dma_start(out=c0_sb[:], in_=c0.rearrange("(m p) h -> p m h", p=P))
+
+        def transpose_x(s, m):
+            x_words = x_raw[:, s, m, :].bitcast(F32)
+            planes = psum.tile([P, HALVES, 2, P], F32, tag="bank")
+            for g in range(HALVES):
+                for u in range(2):
+                    nc.tensor.transpose(
+                        planes[:, g, u, :],
+                        x_words[:, 2 * P * g + u : 2 * P * (g + 1) : 2],
+                        ident[:],
+                    )
+            return planes
+
+        def regroup_x(engine_copy, s, m, planes):
+            dst = x_grouped[:, m, HALVES * s : HALVES * (s + 1), :].bitcast(F32)
+            engine_copy(
+                out=dst.rearrange("p g (r u) -> p g r u", u=2),
+                in_=planes[:].rearrange("p g u r -> p g r u"),
+            )
+
+        def quantise_x(s, m):
+            both = slice(HALVES * s, HALVES * (s + 1))
+            nc.vector.quantize_mx(
+                out=x_codes[:, m, both, :].rearrange("p g r -> p (g r)").bitcast(FP8X4),
+                scales=x_scales[:, m, both, :].rearrange("p g r -> p (g r)"),
+                in_=x_grouped[:, m, both, :].rearrange("p g w -> p (g w)"),
+            )
+
+        blocks = [(s, m) for s in range(2) for m in range(M_TILES)]
+        for b in range(len(blocks) + 1):
+            if b < len(blocks):
+                s, m = blocks[b]
+                planes = transpose_x(s, m)
+                regroup_x(nc.scalar.copy if b % 2 == 0 else nc.vector.tensor_copy, s, m, planes)
+            if b >= 1:
+                quantise_x(*blocks[b - 1])
+
+        nc.vector.tensor_tensor(
+            out=bias_pick[:], in0=ident[:, 0:CHUNKS], in1=ident[:, CHUNKS : 2 * CHUNKS], op=ADD
+        )
+        for n in range(CHUNKS):
+            spread = psum.tile([P, HS], F32, tag="bank")
+            nc.tensor.matmul(
+                spread[:],
+                lhsT=bias_pick[:, n : n + 1].to_broadcast([P, P]),
+                rhs=bias_rows[:],
+                start=True,
+                stop=True,
+            )
+            if n % 2 == 0:
+                nc.scalar.copy(out=bias_sb[:, n, :], in_=spread[:])
+            else:
+                nc.vector.tensor_copy(out=bias_sb[:, n, :], in_=spread[:])
+
+        gate_sb = {}
+        cell_sb = {}
+
+        def gate_block(j, gate, m):
+            n = GATES * j + gate
+            cols = slice(HS * n, HS * (n + 1))
+            acc = psum.tile([P, HS], F32, tag="bank")
+            for c in range(PASSES):
+                nc.tensor.matmul_mx(
+                    out=acc[:],
+                    lhsT=x_codes[:, m, c, :].bitcast(FP8X4),
+                    lhsT_scale=x_scales[:, m, c, :],
+                    rhs=w_codes[:, c, cols].bitcast(FP8X4),
+                    rhs_scale=w_planes[4 * c : P, cols],
+                    start=(c == 0),
+                    stop=(c == PASSES - 1),
+                )
+            act = work.tile([P, HS], F32, tag="gate%d" % gate)
+            nc.vector.tensor_tensor(out=act[:], in0=acc[:], in1=bias_sb[:, n, :], op=ADD)
+            nc.scalar.activation(out=act[:], in_=act[:], func=TANH if gate == 0 else SIGMOID)
+            gate_sb[(j, gate, m)] = act
+
+        def gate_products(j, gate, m):
+            rows = slice(P * m, P * (m + 1))
+            cols = slice(HS * j, HS * (j + 1))
+            if gate == 1:
+                g_act = gate_sb[(j, 0, m)]
+                nc.gpsimd.tensor_tensor(out=g_act[:], in0=g_act[:], in1=gate_sb[(j, 1, m)][:], op=MULT)
+            if gate == 2:
+                f_act = gate_sb[(j, 2, m)]
+                nc.gpsimd.tensor_tensor(out=f_act[:], in0=f_act[:], in1=c0_sb[:, m, cols], op=MULT)
+                c1 = work.tile([P, HS], F32, tag="c1")
+                nc.vector.tensor_tensor(out=c1[:], in0=gate_sb[(j, 0, m)][:], in1=f_act[:], op=ADD)
+                nc.sync.dma_start(out=c1_out[rows, cols], in_=c1[:])
+                tanh_c1 = work.tile([P, HS], F32, tag="tanh_c1")
+                nc.scalar.activation(out=tanh_c1[:], in_=c1[:], func=TANH)
+                cell_sb[(j, m)] = tanh_c1
+            if gate == 3:
+                o_act = gate_sb[(j, 3, m)]
+                nc.vector.tensor_tensor(out=o_act[:], in0=o_act[:], in1=cell_sb[(j, m)][:], op=MULT)
+                nc.sync.dma_start(out=h1_out[rows, cols], in_=o_act[:])
+
+        steps = [(j, gate, m) for j in range(GROUPS) for gate in range(GATES) for m in range(M_TILES)]
+        for q in range(STEPS + LAG):
+            if q < STEPS:
+                gate_block(*steps[q])
+            if q >= LAG:
+                gate_products(*steps[q - LAG])

@@ -192,10 +192,10 @@ def tile_symlstmcell_kernel(
             cols = slice(HS * j, HS * (j + 1))
             if gate == 1:
                 g_act = gate_sb[(j, 0, m)]
-                nc.gpsimd.tensor_tensor(out=g_act[:], in0=g_act[:], in1=gate_sb[(j, 1, m)][:], op=MULT)
+                nc.vector.tensor_tensor(out=g_act[:], in0=g_act[:], in1=gate_sb[(j, 1, m)][:], op=MULT)
             if gate == 2:
                 f_act = gate_sb[(j, 2, m)]
-                nc.gpsimd.tensor_tensor(out=f_act[:], in0=f_act[:], in1=c0_sb[:, m, cols], op=MULT)
+                nc.vector.tensor_tensor(out=f_act[:], in0=f_act[:], in1=c0_sb[:, m, cols], op=MULT)
                 c1 = work.tile([P, HS], F32, tag="c1")
                 nc.vector.tensor_tensor(out=c1[:], in0=gate_sb[(j, 0, m)][:], in1=f_act[:], op=ADD)
                 nc.sync.dma_start(out=c1_out[rows, cols], in_=c1[:])

@@ -27,7 +27,6 @@ GROUPS = 2
 CHUNKS = GROUPS * GATES
 GATE_COLS = CHUNKS * HS
 STEPS = CHUNKS * M_TILES
-LAG = 2
 
 FLOPS = 2 * BATCH * (2 * WIDTH) * GATE_COLS
 
@@ -52,6 +51,7 @@ def tile_symlstmcell_kernel(
     scales = (w_ih_scales, w_hh_scales)
 
     with ExitStack() as ctx:
+        ctx.enter_context(tc.manual_schedule())
         keep = ctx.enter_context(tc.tile_pool(name="keep", bufs=1))
         work = ctx.enter_context(tc.tile_pool(name="work", bufs=M_TILES))
         psum = ctx.enter_context(tc.psum_pool(name="psum", bufs=8))
@@ -68,12 +68,6 @@ def tile_symlstmcell_kernel(
         bias_sb = keep.tile([P, CHUNKS, HS], F32)
         ident = keep.tile([P, P], F32)
         warm = keep.tile([P, 1], F32)
-
-        nc.vector.memset(w_planes[:].bitcast(I32), 0)
-        nc.vector.memset(bias_rows[:], 0.0)
-        nc.vector.memset(warm[:], 0.0)
-        make_identity(nc, ident[:])
-        nc.scalar.activation(out=warm[:], in_=warm[:], func=SIGMOID)
 
         def load_weight_scales(s):
             for quad in range(4):
@@ -97,6 +91,11 @@ def tile_symlstmcell_kernel(
                 in_=all_words[:, :, HS * n : HS * (n + 1)],
             )
 
+        nc.vector.memset(w_planes[:].bitcast(I32), 0)
+        nc.vector.memset(bias_rows[:], 0.0)
+        nc.vector.memset(warm[:], 0.0)
+        make_identity(nc, ident[:])
+
         load_weight_scales(0)
         for s in range(2):
             for half in range(2):
@@ -111,6 +110,11 @@ def tile_symlstmcell_kernel(
                 load_weight_chunk(s, n)
             if n == 1:
                 nc.sync.dma_start(out=c0_sb[:], in_=c0.rearrange("(m p) h -> p m h", p=P))
+
+        nc.scalar.activation(out=warm[:], in_=warm[:], func=SIGMOID)
+        nc.vector.tensor_tensor(
+            out=bias_pick[:], in0=ident[:, 0:CHUNKS], in1=ident[:, CHUNKS : 2 * CHUNKS], op=ADD
+        )
 
         def transpose_x(s, m):
             x_words = x_raw[:, s, m, :].bitcast(F32)
@@ -148,9 +152,6 @@ def tile_symlstmcell_kernel(
             if b >= 1:
                 quantise_x(*blocks[b - 1])
 
-        nc.vector.tensor_tensor(
-            out=bias_pick[:], in0=ident[:, 0:CHUNKS], in1=ident[:, CHUNKS : 2 * CHUNKS], op=ADD
-        )
         for n in range(CHUNKS):
             spread = psum.tile([P, HS], F32, tag="bank")
             nc.tensor.matmul(
@@ -187,29 +188,39 @@ def tile_symlstmcell_kernel(
             nc.scalar.activation(out=act[:], in_=act[:], func=TANH if gate == 0 else SIGMOID)
             gate_sb[(j, gate, m)] = act
 
+        def combine(out, in0, in1, op):
+            nc.vector.tensor_tensor(out=out, in0=in0, in1=in1, op=op)
+
         def gate_products(j, gate, m):
-            rows = slice(P * m, P * (m + 1))
-            cols = slice(HS * j, HS * (j + 1))
             if gate == 1:
                 g_act = gate_sb[(j, 0, m)]
-                nc.vector.tensor_tensor(out=g_act[:], in0=g_act[:], in1=gate_sb[(j, 1, m)][:], op=MULT)
+                combine(g_act[:], g_act[:], gate_sb[(j, 1, m)][:], MULT)
             if gate == 2:
                 f_act = gate_sb[(j, 2, m)]
-                nc.vector.tensor_tensor(out=f_act[:], in0=f_act[:], in1=c0_sb[:, m, cols], op=MULT)
+                combine(f_act[:], f_act[:], c0_sb[:, m, HS * j : HS * (j + 1)], MULT)
+            if gate == 3:
+                o_act = gate_sb[(j, 3, m)]
+                combine(o_act[:], o_act[:], cell_sb[(j, m)][:], MULT)
+                nc.sync.dma_start(
+                    out=h1_out[P * m : P * (m + 1), HS * j : HS * (j + 1)], in_=o_act[:]
+                )
+
+        def cell_update(j, gate, m):
+            if gate == 2:
                 c1 = work.tile([P, HS], F32, tag="c1")
-                nc.vector.tensor_tensor(out=c1[:], in0=gate_sb[(j, 0, m)][:], in1=f_act[:], op=ADD)
-                nc.sync.dma_start(out=c1_out[rows, cols], in_=c1[:])
+                combine(c1[:], gate_sb[(j, 0, m)][:], gate_sb[(j, 2, m)][:], ADD)
+                nc.sync.dma_start(
+                    out=c1_out[P * m : P * (m + 1), HS * j : HS * (j + 1)], in_=c1[:]
+                )
                 tanh_c1 = work.tile([P, HS], F32, tag="tanh_c1")
                 nc.scalar.activation(out=tanh_c1[:], in_=c1[:], func=TANH)
                 cell_sb[(j, m)] = tanh_c1
-            if gate == 3:
-                o_act = gate_sb[(j, 3, m)]
-                nc.vector.tensor_tensor(out=o_act[:], in0=o_act[:], in1=cell_sb[(j, m)][:], op=MULT)
-                nc.sync.dma_start(out=h1_out[rows, cols], in_=o_act[:])
 
         steps = [(j, gate, m) for j in range(GROUPS) for gate in range(GATES) for m in range(M_TILES)]
-        for q in range(STEPS + LAG):
+        for q in range(STEPS + 2):
             if q < STEPS:
                 gate_block(*steps[q])
-            if q >= LAG:
-                gate_products(*steps[q - LAG])
+            if q >= 2:
+                cell_update(*steps[q - 2])
+            if 1 <= q <= STEPS:
+                gate_products(*steps[q - 1])

@@ -69,20 +69,21 @@ def tile_symlstmcell_kernel(
         ident = keep.tile([P, P], F32)
         warm = keep.tile([P, 1], F32)
 
-        def load_weight_scales(s):
-            for quad in range(4):
-                first = 32 * quad + 4 * HALVES * s
-                nc.sync.dma_start(
-                    out=w_planes[first : first + 4 * HALVES, :].bitcast(I32),
-                    in_=scales[s][:, 4 * quad : 4 * quad + 4, :].bitcast(I32),
-                )
-
         def load_x(s, half):
             rows = sources[s][2 * P * half : 2 * P * (half + 1), :]
-            nc.scalar.dma_start(
+            nc.sync.dma_start(
                 out=x_raw[:, s, 2 * half : 2 * half + 2, :],
                 in_=rows.rearrange("(m p) k -> p m k", p=P),
             )
+
+        def load_weight_scales(s, j):
+            cols = slice(GATES * HS * j, GATES * HS * (j + 1))
+            for quad in range(4):
+                first = 32 * quad + 4 * HALVES * s
+                nc.sync.dma_start(
+                    out=w_planes[first : first + 4 * HALVES, cols].bitcast(I32),
+                    in_=scales[s][:, 4 * quad : 4 * quad + 4, cols].bitcast(I32),
+                )
 
         def load_weight_chunk(s, n):
             all_words = words[s].rearrange("g p n t -> p g (n t)").bitcast(I32)
@@ -96,20 +97,27 @@ def tile_symlstmcell_kernel(
         nc.vector.memset(warm[:], 0.0)
         make_identity(nc, ident[:])
 
-        load_weight_scales(0)
         for s in range(2):
             for half in range(2):
                 load_x(s, half)
-        load_weight_scales(1)
+        load_weight_scales(0, 0)
+        for s in range(2):
+            load_weight_chunk(s, 0)
+        load_weight_scales(1, 0)
+        for s in range(2):
+            load_weight_chunk(s, 1)
+        nc.sync.dma_start(out=c0_sb[:], in_=c0.rearrange("(m p) h -> p m h", p=P))
+        for s in range(2):
+            load_weight_chunk(s, 2)
+        for s in range(2):
+            load_weight_scales(s, 1)
+        for n in range(3, CHUNKS):
+            for s in range(2):
+                load_weight_chunk(s, n)
         nc.gpsimd.dma_start(out=bias_rows[0:CHUNKS, :], in_=bias_ih.rearrange("(n c) -> n c", c=HS))
         nc.gpsimd.dma_start(
             out=bias_rows[CHUNKS : 2 * CHUNKS, :], in_=bias_hh.rearrange("(n c) -> n c", c=HS)
         )
-        for n in range(CHUNKS):
-            for s in range(2):
-                load_weight_chunk(s, n)
-            if n == 1:
-                nc.sync.dma_start(out=c0_sb[:], in_=c0.rearrange("(m p) h -> p m h", p=P))
 
         nc.scalar.activation(out=warm[:], in_=warm[:], func=SIGMOID)
         nc.vector.tensor_tensor(

@@ -27,6 +27,10 @@ GROUPS = 2
 CHUNKS = GROUPS * GATES
 GATE_COLS = CHUNKS * HS
 STEPS = CHUNKS * M_TILES
+BIAS_W = 256
+BIAS_ROWS = GATE_COLS // BIAS_W
+WARM_UP = 4
+V_COLS = 384
 
 FLOPS = 2 * BATCH * (2 * WIDTH) * GATE_COLS
 
@@ -63,8 +67,8 @@ def tile_symlstmcell_kernel(
         w_codes = keep.tile([P, PASSES, GATE_COLS], U32, align_bytes=64)
         w_planes = keep.tile([P, GATE_COLS], U8, align_bytes=64)
         c0_sb = keep.tile([P, M_TILES, WIDTH], BF16)
-        bias_rows = keep.tile([P, HS], BF16)
-        bias_pick = keep.tile([P, CHUNKS], BF16)
+        bias_rows = keep.tile([P, BIAS_W], BF16)
+        bias_pick = keep.tile([P, BIAS_ROWS], BF16)
         bias_sb = keep.tile([P, CHUNKS, HS], F32)
         ident = keep.tile([P, P], F32)
         warm = keep.tile([P, 1], F32)
@@ -93,9 +97,17 @@ def tile_symlstmcell_kernel(
             )
 
         nc.vector.memset(w_planes[:].bitcast(I32), 0)
-        nc.vector.memset(bias_rows[:], 0.0)
         nc.vector.memset(warm[:], 0.0)
         make_identity(nc, ident[:])
+
+        nc.sync.dma_start(
+            out=bias_rows[0:BIAS_ROWS, :], in_=bias_ih.rearrange("(v c) -> v c", c=BIAS_W)
+        )
+        nc.sync.dma_start(
+            out=bias_rows[BIAS_ROWS : 2 * BIAS_ROWS, :], in_=bias_hh.rearrange("(v c) -> v c", c=BIAS_W)
+        )
+        nc.vector.memset(bias_rows[32:64, :], 0.0)
+        nc.vector.memset(bias_rows[64:128, :], 0.0)
 
         for s in range(2):
             for half in range(2):
@@ -114,14 +126,10 @@ def tile_symlstmcell_kernel(
         for n in range(3, CHUNKS):
             for s in range(2):
                 load_weight_chunk(s, n)
-        nc.gpsimd.dma_start(out=bias_rows[0:CHUNKS, :], in_=bias_ih.rearrange("(n c) -> n c", c=HS))
-        nc.gpsimd.dma_start(
-            out=bias_rows[CHUNKS : 2 * CHUNKS, :], in_=bias_hh.rearrange("(n c) -> n c", c=HS)
-        )
 
         nc.scalar.activation(out=warm[:], in_=warm[:], func=SIGMOID)
         nc.vector.tensor_tensor(
-            out=bias_pick[:], in0=ident[:, 0:CHUNKS], in1=ident[:, CHUNKS : 2 * CHUNKS], op=ADD
+            out=bias_pick[:], in0=ident[:, 0:BIAS_ROWS], in1=ident[:, BIAS_ROWS : 2 * BIAS_ROWS], op=ADD
         )
 
         def transpose_x(s, m):
@@ -151,28 +159,31 @@ def tile_symlstmcell_kernel(
                 in_=x_grouped[:, m, both, :].rearrange("p g w -> p (g w)"),
             )
 
+        def spread_bias(n):
+            spread = psum.tile([P, HS], F32, tag="bank")
+            for part in range(HS // BIAS_W):
+                v = (HS // BIAS_W) * n + part
+                nc.tensor.matmul(
+                    spread[:, BIAS_W * part : BIAS_W * (part + 1)],
+                    lhsT=bias_pick[:, v : v + 1].to_broadcast([P, P]),
+                    rhs=bias_rows[:],
+                    start=True,
+                    stop=True,
+                )
+            nc.scalar.copy(out=bias_sb[:, n, :], in_=spread[:])
+
+        for n in range(WARM_UP):
+            spread_bias(n)
         blocks = [(s, m) for s in range(2) for m in range(M_TILES)]
         for b in range(len(blocks) + 1):
             if b < len(blocks):
                 s, m = blocks[b]
                 planes = transpose_x(s, m)
                 regroup_x(nc.scalar.copy if b % 2 == 0 else nc.vector.tensor_copy, s, m, planes)
+                if b % 2 == 1:
+                    spread_bias(WARM_UP + b // 2)
             if b >= 1:
                 quantise_x(*blocks[b - 1])
-
-        for n in range(CHUNKS):
-            spread = psum.tile([P, HS], F32, tag="bank")
-            nc.tensor.matmul(
-                spread[:],
-                lhsT=bias_pick[:, n : n + 1].to_broadcast([P, P]),
-                rhs=bias_rows[:],
-                start=True,
-                stop=True,
-            )
-            if n % 2 == 0:
-                nc.scalar.copy(out=bias_sb[:, n, :], in_=spread[:])
-            else:
-                nc.vector.tensor_copy(out=bias_sb[:, n, :], in_=spread[:])
 
         gate_sb = {}
         cell_sb = {}
@@ -197,7 +208,8 @@ def tile_symlstmcell_kernel(
             gate_sb[(j, gate, m)] = act
 
         def combine(out, in0, in1, op):
-            nc.vector.tensor_tensor(out=out, in0=in0, in1=in1, op=op)
+            nc.vector.tensor_tensor(out=out[:, :V_COLS], in0=in0[:, :V_COLS], in1=in1[:, :V_COLS], op=op)
+            nc.gpsimd.tensor_tensor(out=out[:, V_COLS:], in0=in0[:, V_COLS:], in1=in1[:, V_COLS:], op=op)
 
         def gate_products(j, gate, m):
             if gate == 1:

@@ -22,15 +22,16 @@ K_PASS = 4 * P
 HALVES = WIDTH // K_PASS
 PASSES = 2 * HALVES
 HS = 512
+G, I, F, O = 0, 1, 2, 3
 GATES = 4
 GROUPS = 2
 CHUNKS = GROUPS * GATES
 GATE_COLS = CHUNKS * HS
-STEPS = CHUNKS * M_TILES
 BIAS_W = 256
 BIAS_ROWS = GATE_COLS // BIAS_W
 WARM_UP = 4
-V_COLS = 384
+PRODUCT_LAG = 2
+CELL_LAG = 3
 
 FLOPS = 2 * BATCH * (2 * WIDTH) * GATE_COLS
 
@@ -54,6 +55,14 @@ def tile_symlstmcell_kernel(
     words = (w_ih_words, w_hh_words)
     scales = (w_ih_scales, w_hh_scales)
 
+    steps = []
+    for j in range(GROUPS):
+        steps += [(j, F, m) for m in range(M_TILES)]
+        for m in range(M_TILES):
+            steps += [(j, G, m), (j, I, m)]
+        steps += [(j, O, m) for m in range(M_TILES)]
+    chunk_order = [GATES * j + gate for (j, gate, m) in steps if m == 0]
+
     with ExitStack() as ctx:
         ctx.enter_context(tc.manual_schedule())
         keep = ctx.enter_context(tc.tile_pool(name="keep", bufs=1))
@@ -66,7 +75,7 @@ def tile_symlstmcell_kernel(
         x_scales = keep.tile([P, M_TILES, PASSES, P], U8, align_bytes=64)
         w_codes = keep.tile([P, PASSES, GATE_COLS], U32, align_bytes=64)
         w_planes = keep.tile([P, GATE_COLS], U8, align_bytes=64)
-        c0_sb = keep.tile([P, M_TILES, WIDTH], BF16)
+        c0_sb = keep.tile([P, GROUPS, M_TILES, HS], BF16)
         bias_rows = keep.tile([P, BIAS_W], BF16)
         bias_pick = keep.tile([P, BIAS_ROWS], BF16)
         bias_sb = keep.tile([P, CHUNKS, HS], F32)
@@ -89,16 +98,19 @@ def tile_symlstmcell_kernel(
                     in_=scales[s][:, 4 * quad : 4 * quad + 4, cols].bitcast(I32),
                 )
 
-        def load_weight_chunk(s, n):
-            all_words = words[s].rearrange("g p n t -> p g (n t)").bitcast(I32)
-            nc.sync.dma_start(
-                out=w_codes[:, HALVES * s : HALVES * (s + 1), HS * n : HS * (n + 1)].bitcast(I32),
-                in_=all_words[:, :, HS * n : HS * (n + 1)],
-            )
+        def load_weight_chunk(n):
+            for s in range(2):
+                all_words = words[s].rearrange("g p n t -> p g (n t)").bitcast(I32)
+                nc.sync.dma_start(
+                    out=w_codes[:, HALVES * s : HALVES * (s + 1), HS * n : HS * (n + 1)].bitcast(I32),
+                    in_=all_words[:, :, HS * n : HS * (n + 1)],
+                )
 
-        nc.vector.memset(w_planes[:].bitcast(I32), 0)
-        nc.vector.memset(warm[:], 0.0)
-        make_identity(nc, ident[:])
+        def load_c0(j):
+            nc.sync.dma_start(
+                out=c0_sb[:, j, :, :],
+                in_=c0[:, HS * j : HS * (j + 1)].rearrange("(m p) h -> p m h", p=P),
+            )
 
         nc.sync.dma_start(
             out=bias_rows[0:BIAS_ROWS, :], in_=bias_ih.rearrange("(v c) -> v c", c=BIAS_W)
@@ -108,29 +120,39 @@ def tile_symlstmcell_kernel(
         )
         nc.vector.memset(bias_rows[32:64, :], 0.0)
         nc.vector.memset(bias_rows[64:128, :], 0.0)
+        nc.vector.memset(w_planes[:].bitcast(I32), 0)
+        nc.vector.memset(warm[:], 0.0)
+        make_identity(nc, ident[:])
 
         for s in range(2):
             for half in range(2):
                 load_x(s, half)
-        load_weight_scales(0, 0)
-        for s in range(2):
-            load_weight_chunk(s, 0)
-        load_weight_scales(1, 0)
-        for s in range(2):
-            load_weight_chunk(s, 1)
-        nc.sync.dma_start(out=c0_sb[:], in_=c0.rearrange("(m p) h -> p m h", p=P))
-        for s in range(2):
-            load_weight_chunk(s, 2)
-        for s in range(2):
-            load_weight_scales(s, 1)
-        for n in range(3, CHUNKS):
-            for s in range(2):
-                load_weight_chunk(s, n)
+        for j in range(GROUPS):
+            first_chunk = chunk_order[GATES * j]
+            load_weight_scales(0, j)
+            load_weight_chunk(first_chunk)
+            load_weight_scales(1, j)
+            load_c0(j)
+            for n in chunk_order[GATES * j + 1 : GATES * (j + 1)]:
+                load_weight_chunk(n)
 
         nc.scalar.activation(out=warm[:], in_=warm[:], func=SIGMOID)
         nc.vector.tensor_tensor(
             out=bias_pick[:], in0=ident[:, 0:BIAS_ROWS], in1=ident[:, BIAS_ROWS : 2 * BIAS_ROWS], op=ADD
         )
+
+        def spread_bias(n):
+            spread = psum.tile([P, HS], F32, tag="bank")
+            for part in range(HS // BIAS_W):
+                v = (HS // BIAS_W) * n + part
+                nc.tensor.matmul(
+                    spread[:, BIAS_W * part : BIAS_W * (part + 1)],
+                    lhsT=bias_pick[:, v : v + 1].to_broadcast([P, P]),
+                    rhs=bias_rows[:],
+                    start=True,
+                    stop=True,
+                )
+            nc.scalar.copy(out=bias_sb[:, n, :], in_=spread[:])
 
         def transpose_x(s, m):
             x_words = x_raw[:, s, m, :].bitcast(F32)
@@ -159,20 +181,7 @@ def tile_symlstmcell_kernel(
                 in_=x_grouped[:, m, both, :].rearrange("p g w -> p (g w)"),
             )
 
-        def spread_bias(n):
-            spread = psum.tile([P, HS], F32, tag="bank")
-            for part in range(HS // BIAS_W):
-                v = (HS // BIAS_W) * n + part
-                nc.tensor.matmul(
-                    spread[:, BIAS_W * part : BIAS_W * (part + 1)],
-                    lhsT=bias_pick[:, v : v + 1].to_broadcast([P, P]),
-                    rhs=bias_rows[:],
-                    start=True,
-                    stop=True,
-                )
-            nc.scalar.copy(out=bias_sb[:, n, :], in_=spread[:])
-
-        for n in range(WARM_UP):
+        for n in chunk_order[:WARM_UP]:
             spread_bias(n)
         blocks = [(s, m) for s in range(2) for m in range(M_TILES)]
         for b in range(len(blocks) + 1):
@@ -181,7 +190,7 @@ def tile_symlstmcell_kernel(
                 planes = transpose_x(s, m)
                 regroup_x(nc.scalar.copy if b % 2 == 0 else nc.vector.tensor_copy, s, m, planes)
                 if b % 2 == 1:
-                    spread_bias(WARM_UP + b // 2)
+                    spread_bias(chunk_order[WARM_UP + b // 2])
             if b >= 1:
                 quantise_x(*blocks[b - 1])
 
@@ -204,43 +213,34 @@ def tile_symlstmcell_kernel(
                 )
             act = work.tile([P, HS], F32, tag="gate%d" % gate)
             nc.vector.tensor_tensor(out=act[:], in0=acc[:], in1=bias_sb[:, n, :], op=ADD)
-            nc.scalar.activation(out=act[:], in_=act[:], func=TANH if gate == 0 else SIGMOID)
+            nc.scalar.activation(out=act[:], in_=act[:], func=TANH if gate == G else SIGMOID)
             gate_sb[(j, gate, m)] = act
 
-        def combine(out, in0, in1, op):
-            nc.vector.tensor_tensor(out=out[:, :V_COLS], in0=in0[:, :V_COLS], in1=in1[:, :V_COLS], op=op)
-            nc.gpsimd.tensor_tensor(out=out[:, V_COLS:], in0=in0[:, V_COLS:], in1=in1[:, V_COLS:], op=op)
-
-        def gate_products(j, gate, m):
-            if gate == 1:
-                g_act = gate_sb[(j, 0, m)]
-                combine(g_act[:], g_act[:], gate_sb[(j, 1, m)][:], MULT)
-            if gate == 2:
-                f_act = gate_sb[(j, 2, m)]
-                combine(f_act[:], f_act[:], c0_sb[:, m, HS * j : HS * (j + 1)], MULT)
-            if gate == 3:
-                o_act = gate_sb[(j, 3, m)]
-                combine(o_act[:], o_act[:], cell_sb[(j, m)][:], MULT)
-                nc.sync.dma_start(
-                    out=h1_out[P * m : P * (m + 1), HS * j : HS * (j + 1)], in_=o_act[:]
-                )
+        def gate_product(j, gate, m):
+            act = gate_sb[(j, gate, m)]
+            if gate == F:
+                nc.vector.tensor_tensor(out=act[:], in0=act[:], in1=c0_sb[:, j, m, :], op=MULT)
+            if gate == I:
+                nc.vector.tensor_tensor(out=act[:], in0=act[:], in1=gate_sb[(j, G, m)][:], op=MULT)
+            if gate == O:
+                nc.vector.tensor_tensor(out=act[:], in0=act[:], in1=cell_sb[(j, m)][:], op=MULT)
+                nc.sync.dma_start(out=h1_out[P * m : P * (m + 1), HS * j : HS * (j + 1)], in_=act[:])
 
         def cell_update(j, gate, m):
-            if gate == 2:
+            if gate == I:
                 c1 = work.tile([P, HS], F32, tag="c1")
-                combine(c1[:], gate_sb[(j, 0, m)][:], gate_sb[(j, 2, m)][:], ADD)
-                nc.sync.dma_start(
-                    out=c1_out[P * m : P * (m + 1), HS * j : HS * (j + 1)], in_=c1[:]
+                nc.vector.tensor_tensor(
+                    out=c1[:], in0=gate_sb[(j, I, m)][:], in1=gate_sb[(j, F, m)][:], op=ADD
                 )
+                nc.sync.dma_start(out=c1_out[P * m : P * (m + 1), HS * j : HS * (j + 1)], in_=c1[:])
                 tanh_c1 = work.tile([P, HS], F32, tag="tanh_c1")
                 nc.scalar.activation(out=tanh_c1[:], in_=c1[:], func=TANH)
                 cell_sb[(j, m)] = tanh_c1
 
-        steps = [(j, gate, m) for j in range(GROUPS) for gate in range(GATES) for m in range(M_TILES)]
-        for q in range(STEPS + 2):
-            if q < STEPS:
+        for q in range(len(steps) + CELL_LAG):
+            if q < len(steps):
                 gate_block(*steps[q])
-            if q >= 2:
-                cell_update(*steps[q - 2])
-            if 1 <= q <= STEPS:
-                gate_products(*steps[q - 1])
+            if CELL_LAG <= q:
+                cell_update(*steps[q - CELL_LAG])
+            if PRODUCT_LAG <= q < len(steps) + PRODUCT_LAG:
+                gate_product(*steps[q - PRODUCT_LAG])

@@ -32,6 +32,7 @@ BIAS_ROWS = GATE_COLS // BIAS_W
 WARM_UP = 4
 PRODUCT_LAG = 2
 CELL_LAG = 3
+FIRST_C0_LAG = 4
 
 FLOPS = 2 * BATCH * (2 * WIDTH) * GATE_COLS
 
@@ -56,31 +57,37 @@ def tile_symlstmcell_kernel(
     scales = (w_ih_scales, w_hh_scales)
 
     steps = []
-    for j in range(GROUPS):
-        steps += [(j, F, m) for m in range(M_TILES)]
-        for m in range(M_TILES):
-            steps += [(j, G, m), (j, I, m)]
-        steps += [(j, O, m) for m in range(M_TILES)]
+    for gate in (F, G, I, O):
+        steps += [(0, gate, m) for m in range(M_TILES)]
+    steps += [(1, F, m) for m in range(M_TILES)]
+    for m in range(M_TILES):
+        steps += [(1, G, m), (1, I, m)]
+    steps += [(1, O, m) for m in range(M_TILES)]
     chunk_order = [GATES * j + gate for (j, gate, m) in steps if m == 0]
 
     with ExitStack() as ctx:
         ctx.enter_context(tc.manual_schedule())
         keep = ctx.enter_context(tc.tile_pool(name="keep", bufs=1))
         work = ctx.enter_context(tc.tile_pool(name="work", bufs=M_TILES))
-        psum = ctx.enter_context(tc.psum_pool(name="psum", bufs=8))
+        psum = ctx.enter_context(tc.psum_pool(name="psum", bufs=4))
 
         x_raw = keep.tile([P, 2, M_TILES, WIDTH], BF16)
         x_grouped = keep.tile([P, M_TILES, PASSES, 4 * P], BF16, align_bytes=64)
         x_codes = keep.tile([P, M_TILES, PASSES, P], U32, align_bytes=64)
         x_scales = keep.tile([P, M_TILES, PASSES, P], U8, align_bytes=64)
         w_codes = keep.tile([P, PASSES, GATE_COLS], U32, align_bytes=64)
-        w_planes = keep.tile([P, GATE_COLS], U8, align_bytes=64)
+        planes_ih = keep.tile([P, GATE_COLS], U8, align_bytes=64)
+        planes_hh = keep.tile([P, GATE_COLS], U8, align_bytes=64)
+        w_planes = (planes_ih, planes_hh)
         c0_sb = keep.tile([P, GROUPS, M_TILES, HS], BF16)
         bias_rows = keep.tile([P, BIAS_W], BF16)
         bias_pick = keep.tile([P, BIAS_ROWS], BF16)
         bias_sb = keep.tile([P, CHUNKS, HS], F32)
         ident = keep.tile([P, P], F32)
         warm = keep.tile([P, 1], F32)
+
+        def bank(shape, which):
+            return psum.tile(shape, F32, tag="bank_%s" % which, name="bank_%s" % which)
 
         def load_x(s, half):
             rows = sources[s][2 * P * half : 2 * P * (half + 1), :]
@@ -92,19 +99,18 @@ def tile_symlstmcell_kernel(
         def load_weight_scales(s, j):
             cols = slice(GATES * HS * j, GATES * HS * (j + 1))
             for quad in range(4):
-                first = 32 * quad + 4 * HALVES * s
+                first = 32 * quad
                 nc.sync.dma_start(
-                    out=w_planes[first : first + 4 * HALVES, cols].bitcast(I32),
+                    out=w_planes[s][first : first + 4 * HALVES, cols].bitcast(I32),
                     in_=scales[s][:, 4 * quad : 4 * quad + 4, cols].bitcast(I32),
                 )
 
-        def load_weight_chunk(n):
-            for s in range(2):
-                all_words = words[s].rearrange("g p n t -> p g (n t)").bitcast(I32)
-                nc.sync.dma_start(
-                    out=w_codes[:, HALVES * s : HALVES * (s + 1), HS * n : HS * (n + 1)].bitcast(I32),
-                    in_=all_words[:, :, HS * n : HS * (n + 1)],
-                )
+        def load_weight_chunk(n, s):
+            all_words = words[s].rearrange("g p n t -> p g (n t)").bitcast(I32)
+            nc.sync.dma_start(
+                out=w_codes[:, HALVES * s : HALVES * (s + 1), HS * n : HS * (n + 1)].bitcast(I32),
+                in_=all_words[:, :, HS * n : HS * (n + 1)],
+            )
 
         def load_c0(j):
             nc.sync.dma_start(
@@ -112,6 +118,7 @@ def tile_symlstmcell_kernel(
                 in_=c0[:, HS * j : HS * (j + 1)].rearrange("(m p) h -> p m h", p=P),
             )
 
+        nc.vector.memset(planes_ih[:].bitcast(I32), 0)
         nc.sync.dma_start(
             out=bias_rows[0:BIAS_ROWS, :], in_=bias_ih.rearrange("(v c) -> v c", c=BIAS_W)
         )
@@ -120,29 +127,38 @@ def tile_symlstmcell_kernel(
         )
         nc.vector.memset(bias_rows[32:64, :], 0.0)
         nc.vector.memset(bias_rows[64:128, :], 0.0)
-        nc.vector.memset(w_planes[:].bitcast(I32), 0)
+        nc.vector.memset(planes_hh[:].bitcast(I32), 0)
         nc.vector.memset(warm[:], 0.0)
         make_identity(nc, ident[:])
 
+        first_chunk = chunk_order[0]
         for s in range(2):
-            for half in range(2):
-                load_x(s, half)
-        for j in range(GROUPS):
-            first_chunk = chunk_order[GATES * j]
-            load_weight_scales(0, j)
-            load_weight_chunk(first_chunk)
-            load_weight_scales(1, j)
-            load_c0(j)
-            for n in chunk_order[GATES * j + 1 : GATES * (j + 1)]:
-                load_weight_chunk(n)
+            load_x(s, 0)
+            load_x(s, 1)
+            load_weight_scales(s, 0)
+            load_weight_chunk(first_chunk, s)
+        for s in range(2):
+            load_weight_chunk(chunk_order[1], s)
+        load_c0(0)
+        for n in chunk_order[2:GATES]:
+            for s in range(2):
+                load_weight_chunk(n, s)
+        for s in range(2):
+            load_weight_scales(s, 1)
+        for s in range(2):
+            load_weight_chunk(chunk_order[GATES], s)
+        load_c0(1)
+        for n in chunk_order[GATES + 1 :]:
+            for s in range(2):
+                load_weight_chunk(n, s)
 
         nc.scalar.activation(out=warm[:], in_=warm[:], func=SIGMOID)
         nc.vector.tensor_tensor(
             out=bias_pick[:], in0=ident[:, 0:BIAS_ROWS], in1=ident[:, BIAS_ROWS : 2 * BIAS_ROWS], op=ADD
         )
 
-        def spread_bias(n):
-            spread = psum.tile([P, HS], F32, tag="bank")
+        def spread_bias(n, which):
+            spread = bank([P, HS], which)
             for part in range(HS // BIAS_W):
                 v = (HS // BIAS_W) * n + part
                 nc.tensor.matmul(
@@ -154,9 +170,9 @@ def tile_symlstmcell_kernel(
                 )
             nc.scalar.copy(out=bias_sb[:, n, :], in_=spread[:])
 
-        def transpose_x(s, m):
+        def transpose_x(s, m, which):
             x_words = x_raw[:, s, m, :].bitcast(F32)
-            planes = psum.tile([P, HALVES, 2, P], F32, tag="bank")
+            planes = bank([P, HALVES, 2, P], which)
             for g in range(HALVES):
                 for u in range(2):
                     nc.tensor.transpose(
@@ -181,36 +197,52 @@ def tile_symlstmcell_kernel(
                 in_=x_grouped[:, m, both, :].rearrange("p g w -> p (g w)"),
             )
 
-        for n in chunk_order[:WARM_UP]:
-            spread_bias(n)
-        blocks = [(s, m) for s in range(2) for m in range(M_TILES)]
-        for b in range(len(blocks) + 1):
-            if b < len(blocks):
-                s, m = blocks[b]
-                planes = transpose_x(s, m)
-                regroup_x(nc.scalar.copy if b % 2 == 0 else nc.vector.tensor_copy, s, m, planes)
-                if b % 2 == 1:
-                    spread_bias(chunk_order[WARM_UP + b // 2])
-            if b >= 1:
-                quantise_x(*blocks[b - 1])
+        def prepare(s, sets):
+            for m in range(M_TILES):
+                planes = transpose_x(s, m, sets[m % 2])
+                regroup_x(nc.scalar.copy if m % 2 == 0 else nc.vector.tensor_copy, s, m, planes)
+                if m % 2 == 1:
+                    spread_bias(chunk_order[WARM_UP + HALVES * s + m // 2], sets[0])
+                if m >= 1:
+                    quantise_x(s, m - 1)
+            quantise_x(s, M_TILES - 1)
 
-        gate_sb = {}
-        cell_sb = {}
-
-        def gate_block(j, gate, m):
+        def passes(acc, j, gate, m, s):
             n = GATES * j + gate
             cols = slice(HS * n, HS * (n + 1))
-            acc = psum.tile([P, HS], F32, tag="bank")
-            for c in range(PASSES):
+            for g in range(HALVES):
+                c = HALVES * s + g
                 nc.tensor.matmul_mx(
                     out=acc[:],
                     lhsT=x_codes[:, m, c, :].bitcast(FP8X4),
                     lhsT_scale=x_scales[:, m, c, :],
                     rhs=w_codes[:, c, cols].bitcast(FP8X4),
-                    rhs_scale=w_planes[4 * c : P, cols],
+                    rhs_scale=w_planes[s][4 * g : P, cols],
                     start=(c == 0),
                     stop=(c == PASSES - 1),
                 )
+
+        for i, n in enumerate(chunk_order[:WARM_UP]):
+            spread_bias(n, "ab"[i % 2])
+        prepare(0, "ab")
+        open_acc = {}
+        for (j, gate, m) in steps[:M_TILES]:
+            open_acc[m] = bank([P, HS], "a")
+            passes(open_acc[m], j, gate, m, 0)
+        prepare(1, "bb")
+
+        gate_sb = {}
+        cell_sb = {}
+
+        def gate_block(q):
+            j, gate, m = steps[q]
+            n = GATES * j + gate
+            if q < M_TILES:
+                acc = open_acc[m]
+            else:
+                acc = bank([P, HS], "ba"[q % 2])
+                passes(acc, j, gate, m, 0)
+            passes(acc, j, gate, m, 1)
             act = work.tile([P, HS], F32, tag="gate%d" % gate)
             nc.vector.tensor_tensor(out=act[:], in0=acc[:], in1=bias_sb[:, n, :], op=ADD)
             nc.scalar.activation(out=act[:], in_=act[:], func=TANH if gate == G else SIGMOID)
@@ -227,20 +259,26 @@ def tile_symlstmcell_kernel(
                 nc.sync.dma_start(out=h1_out[P * m : P * (m + 1), HS * j : HS * (j + 1)], in_=act[:])
 
         def cell_update(j, gate, m):
-            if gate == I:
-                c1 = work.tile([P, HS], F32, tag="c1")
-                nc.vector.tensor_tensor(
-                    out=c1[:], in0=gate_sb[(j, I, m)][:], in1=gate_sb[(j, F, m)][:], op=ADD
-                )
-                nc.sync.dma_start(out=c1_out[P * m : P * (m + 1), HS * j : HS * (j + 1)], in_=c1[:])
-                tanh_c1 = work.tile([P, HS], F32, tag="tanh_c1")
-                nc.scalar.activation(out=tanh_c1[:], in_=c1[:], func=TANH)
-                cell_sb[(j, m)] = tanh_c1
+            c1 = work.tile([P, HS], F32, tag="c1")
+            nc.vector.tensor_tensor(
+                out=c1[:], in0=gate_sb[(j, I, m)][:], in1=gate_sb[(j, F, m)][:], op=ADD
+            )
+            nc.sync.dma_start(out=c1_out[P * m : P * (m + 1), HS * j : HS * (j + 1)], in_=c1[:])
+            tanh_c1 = work.tile([P, HS], F32, tag="tanh_c1")
+            nc.scalar.activation(out=tanh_c1[:], in_=c1[:], func=TANH)
+            cell_sb[(j, m)] = tanh_c1
 
+        updates = {}
+        products = {}
+        for q, (j, gate, m) in enumerate(steps):
+            lag = FIRST_C0_LAG if (j == 0 and gate == F) else PRODUCT_LAG
+            products.setdefault(q + lag, []).append((j, gate, m))
+            if gate == I:
+                updates.setdefault(q + CELL_LAG, []).append((j, gate, m))
         for q in range(len(steps) + CELL_LAG):
             if q < len(steps):
-                gate_block(*steps[q])
-            if CELL_LAG <= q:
-                cell_update(*steps[q - CELL_LAG])
-            if PRODUCT_LAG <= q < len(steps) + PRODUCT_LAG:
-                gate_product(*steps[q - PRODUCT_LAG])
+                gate_block(q)
+            for block in updates.get(q, []):
+                cell_update(*block)
+            for block in products.get(q, []):
+                gate_product(*block)

@@ -251,7 +251,7 @@ def tile_symlstmcell_kernel(
         def gate_product(j, gate, m):
             act = gate_sb[(j, gate, m)]
             if gate == F:
-                nc.vector.tensor_tensor(out=act[:], in0=act[:], in1=c0_sb[:, j, m, :], op=MULT)
+                nc.gpsimd.tensor_tensor(out=act[:], in0=act[:], in1=c0_sb[:, j, m, :], op=MULT)
             if gate == I:
                 nc.vector.tensor_tensor(out=act[:], in0=act[:], in1=gate_sb[(j, G, m)][:], op=MULT)
             if gate == O:

@@ -32,6 +32,7 @@ BIAS_ROWS = GATE_COLS // BIAS_W
 WARM_UP = 4
 PRODUCT_LAG = 2
 CELL_LAG = 3
+LAST_LAG = 2
 FIRST_C0_LAG = 4
 
 FLOPS = 2 * BATCH * (2 * WIDTH) * GATE_COLS
@@ -69,6 +70,7 @@ def tile_symlstmcell_kernel(
         ctx.enter_context(tc.manual_schedule())
         keep = ctx.enter_context(tc.tile_pool(name="keep", bufs=1))
         work = ctx.enter_context(tc.tile_pool(name="work", bufs=M_TILES))
+        late = ctx.enter_context(tc.tile_pool(name="late", bufs=GROUPS * M_TILES))
         psum = ctx.enter_context(tc.psum_pool(name="psum", bufs=4))
 
         x_raw = keep.tile([P, 2, M_TILES, WIDTH], BF16)
@@ -127,9 +129,12 @@ def tile_symlstmcell_kernel(
         )
         nc.vector.memset(bias_rows[32:64, :], 0.0)
         nc.vector.memset(bias_rows[64:128, :], 0.0)
-        nc.vector.memset(planes_hh[:].bitcast(I32), 0)
         nc.vector.memset(warm[:], 0.0)
         make_identity(nc, ident[:])
+        nc.vector.tensor_tensor(
+            out=bias_pick[:], in0=ident[:, 0:BIAS_ROWS], in1=ident[:, BIAS_ROWS : 2 * BIAS_ROWS], op=ADD
+        )
+        nc.vector.memset(planes_hh[:].bitcast(I32), 0)
 
         first_chunk = chunk_order[0]
         for s in range(2):
@@ -137,27 +142,20 @@ def tile_symlstmcell_kernel(
             load_x(s, 1)
             load_weight_scales(s, 0)
             load_weight_chunk(first_chunk, s)
-        for s in range(2):
-            load_weight_chunk(chunk_order[1], s)
-        load_c0(0)
-        for n in chunk_order[2:GATES]:
+        for position, n in enumerate(chunk_order[1:]):
+            if n == GATES + F:
+                for s in range(2):
+                    load_weight_scales(s, 1)
             for s in range(2):
                 load_weight_chunk(n, s)
-        for s in range(2):
-            load_weight_scales(s, 1)
-        for s in range(2):
-            load_weight_chunk(chunk_order[GATES], s)
-        load_c0(1)
-        for n in chunk_order[GATES + 1 :]:
-            for s in range(2):
-                load_weight_chunk(n, s)
+            if position == 0:
+                load_c0(0)
+            if n == GATES + F:
+                load_c0(1)
 
         nc.scalar.activation(out=warm[:], in_=warm[:], func=SIGMOID)
-        nc.vector.tensor_tensor(
-            out=bias_pick[:], in0=ident[:, 0:BIAS_ROWS], in1=ident[:, BIAS_ROWS : 2 * BIAS_ROWS], op=ADD
-        )
 
-        def spread_bias(n, which):
+        def spread_bias(n, which, engine_copy):
             spread = bank([P, HS], which)
             for part in range(HS // BIAS_W):
                 v = (HS // BIAS_W) * n + part
@@ -168,7 +166,7 @@ def tile_symlstmcell_kernel(
                     start=True,
                     stop=True,
                 )
-            nc.scalar.copy(out=bias_sb[:, n, :], in_=spread[:])
+            engine_copy(out=bias_sb[:, n, :], in_=spread[:])
 
         def transpose_x(s, m, which):
             x_words = x_raw[:, s, m, :].bitcast(F32)
@@ -201,8 +199,6 @@ def tile_symlstmcell_kernel(
             for m in range(M_TILES):
                 planes = transpose_x(s, m, sets[m % 2])
                 regroup_x(nc.scalar.copy if m % 2 == 0 else nc.vector.tensor_copy, s, m, planes)
-                if m % 2 == 1:
-                    spread_bias(chunk_order[WARM_UP + HALVES * s + m // 2], sets[0])
                 if m >= 1:
                     quantise_x(s, m - 1)
             quantise_x(s, M_TILES - 1)
@@ -223,8 +219,10 @@ def tile_symlstmcell_kernel(
                 )
 
         for i, n in enumerate(chunk_order[:WARM_UP]):
-            spread_bias(n, "ab"[i % 2])
+            spread_bias(n, "ab"[i % 2], nc.scalar.copy if i % 2 == 0 else nc.vector.tensor_copy)
         prepare(0, "ab")
+        for n in chunk_order[WARM_UP:]:
+            spread_bias(n, "b", nc.scalar.copy)
         open_acc = {}
         for (j, gate, m) in steps[:M_TILES]:
             open_acc[m] = bank([P, HS], "a")
@@ -243,7 +241,8 @@ def tile_symlstmcell_kernel(
                 acc = bank([P, HS], "ba"[q % 2])
                 passes(acc, j, gate, m, 0)
             passes(acc, j, gate, m, 1)
-            act = work.tile([P, HS], F32, tag="gate%d" % gate)
+            pool = late if gate == O else work
+            act = pool.tile([P, HS], F32, tag="gate%d" % gate, name="act")
             nc.vector.tensor_tensor(out=act[:], in0=acc[:], in1=bias_sb[:, n, :], op=ADD)
             nc.scalar.activation(out=act[:], in_=act[:], func=TANH if gate == G else SIGMOID)
             gate_sb[(j, gate, m)] = act
@@ -264,14 +263,18 @@ def tile_symlstmcell_kernel(
                 out=c1[:], in0=gate_sb[(j, I, m)][:], in1=gate_sb[(j, F, m)][:], op=ADD
             )
             nc.sync.dma_start(out=c1_out[P * m : P * (m + 1), HS * j : HS * (j + 1)], in_=c1[:])
-            tanh_c1 = work.tile([P, HS], F32, tag="tanh_c1")
+            tanh_c1 = late.tile([P, HS], F32, tag="tanh_c1")
             nc.scalar.activation(out=tanh_c1[:], in_=c1[:], func=TANH)
             cell_sb[(j, m)] = tanh_c1
 
         updates = {}
         products = {}
         for q, (j, gate, m) in enumerate(steps):
-            lag = FIRST_C0_LAG if (j == 0 and gate == F) else PRODUCT_LAG
+            lag = PRODUCT_LAG
+            if j == 0 and gate == F:
+                lag = FIRST_C0_LAG
+            if j == 1 and gate == O:
+                lag = LAST_LAG
             products.setdefault(q + lag, []).append((j, gate, m))
             if gate == I:
                 updates.setdefault(q + CELL_LAG, []).append((j, gate, m))

@@ -56,6 +56,8 @@ def tile_symlstmcell_kernel(
     sources = (x_in, h0)
     words = (w_ih_words, w_hh_words)
     scales = (w_ih_scales, w_hh_scales)
+    h1_rows = h1_out.rearrange("(p m) h -> p m h", m=M_TILES)
+    c1_rows = c1_out.rearrange("(p m) h -> p m h", m=M_TILES)
 
     steps = []
     for gate in (F, G, I, O):
@@ -81,7 +83,7 @@ def tile_symlstmcell_kernel(
         planes_ih = keep.tile([P, GATE_COLS], U8, align_bytes=64)
         planes_hh = keep.tile([P, GATE_COLS], U8, align_bytes=64)
         w_planes = (planes_ih, planes_hh)
-        c0_sb = keep.tile([P, GROUPS, M_TILES, HS], BF16)
+        c0_sb = keep.tile([P, M_TILES, WIDTH], BF16)
         bias_rows = keep.tile([P, BIAS_W], BF16)
         bias_pick = keep.tile([P, BIAS_ROWS], BF16)
         bias_sb = keep.tile([P, CHUNKS, HS], F32)
@@ -92,10 +94,10 @@ def tile_symlstmcell_kernel(
             return psum.tile(shape, F32, tag="bank_%s" % which, name="bank_%s" % which)
 
         def load_x(s, half):
-            rows = sources[s][2 * P * half : 2 * P * (half + 1), :]
+            rows = sources[s].rearrange("(p m) k -> p m k", m=M_TILES)
             nc.sync.dma_start(
                 out=x_raw[:, s, 2 * half : 2 * half + 2, :],
-                in_=rows.rearrange("(m p) k -> p m k", p=P),
+                in_=rows[:, 2 * half : 2 * half + 2, :],
             )
 
         def load_weight_scales(s, j):
@@ -114,10 +116,11 @@ def tile_symlstmcell_kernel(
                 in_=all_words[:, :, HS * n : HS * (n + 1)],
             )
 
-        def load_c0(j):
+        def load_c0(half):
+            rows = c0.rearrange("(p m) h -> p m h", m=M_TILES)
             nc.sync.dma_start(
-                out=c0_sb[:, j, :, :],
-                in_=c0[:, HS * j : HS * (j + 1)].rearrange("(m p) h -> p m h", p=P),
+                out=c0_sb[:, 2 * half : 2 * half + 2, :],
+                in_=rows[:, 2 * half : 2 * half + 2, :],
             )
 
         nc.vector.memset(planes_ih[:].bitcast(I32), 0)
@@ -148,10 +151,8 @@ def tile_symlstmcell_kernel(
                     load_weight_scales(s, 1)
             for s in range(2):
                 load_weight_chunk(n, s)
-            if position == 0:
-                load_c0(0)
-            if n == GATES + F:
-                load_c0(1)
+            if position < 2:
+                load_c0(position)
 
         nc.scalar.activation(out=warm[:], in_=warm[:], func=SIGMOID)
 
@@ -250,19 +251,19 @@ def tile_symlstmcell_kernel(
         def gate_product(j, gate, m):
             act = gate_sb[(j, gate, m)]
             if gate == F:
-                nc.gpsimd.tensor_tensor(out=act[:], in0=act[:], in1=c0_sb[:, j, m, :], op=MULT)
+                nc.gpsimd.tensor_tensor(out=act[:], in0=act[:], in1=c0_sb[:, m, HS * j : HS * (j + 1)], op=MULT)
             if gate == I:
                 nc.vector.tensor_tensor(out=act[:], in0=act[:], in1=gate_sb[(j, G, m)][:], op=MULT)
             if gate == O:
                 nc.vector.tensor_tensor(out=act[:], in0=act[:], in1=cell_sb[(j, m)][:], op=MULT)
-                nc.sync.dma_start(out=h1_out[P * m : P * (m + 1), HS * j : HS * (j + 1)], in_=act[:])
+                nc.sync.dma_start(out=h1_rows[:, m, HS * j : HS * (j + 1)], in_=act[:])
 
         def cell_update(j, gate, m):
             c1 = work.tile([P, HS], F32, tag="c1")
             nc.vector.tensor_tensor(
                 out=c1[:], in0=gate_sb[(j, I, m)][:], in1=gate_sb[(j, F, m)][:], op=ADD
             )
-            nc.sync.dma_start(out=c1_out[P * m : P * (m + 1), HS * j : HS * (j + 1)], in_=c1[:])
+            nc.sync.dma_start(out=c1_rows[:, m, HS * j : HS * (j + 1)], in_=c1[:])
             tanh_c1 = late.tile([P, HS], F32, tag="tanh_c1")
             nc.scalar.activation(out=tanh_c1[:], in_=c1[:], func=TANH)
             cell_sb[(j, m)] = tanh_c1

@@ -32,7 +32,7 @@ BIAS_ROWS = GATE_COLS // BIAS_W
 WARM_UP = 4
 PRODUCT_LAG = 2
 CELL_LAG = 3
-LAST_LAG = 2
+LAST_LAG = 1
 FIRST_C0_LAG = 4
 
 FLOPS = 2 * BATCH * (2 * WIDTH) * GATE_COLS
@@ -60,12 +60,13 @@ def tile_symlstmcell_kernel(
     c1_rows = c1_out.rearrange("(p m) h -> p m h", m=M_TILES)
 
     steps = []
-    for gate in (F, G, I, O):
+    for gate in (F, G, I):
         steps += [(0, gate, m) for m in range(M_TILES)]
     steps += [(1, F, m) for m in range(M_TILES)]
     for m in range(M_TILES):
         steps += [(1, G, m), (1, I, m)]
-    steps += [(1, O, m) for m in range(M_TILES)]
+    for j in range(GROUPS):
+        steps += [(j, O, m) for m in range(M_TILES)]
     chunk_order = [GATES * j + gate for (j, gate, m) in steps if m == 0]
 
     with ExitStack() as ctx:
@@ -255,7 +256,8 @@ def tile_symlstmcell_kernel(
             if gate == I:
                 nc.vector.tensor_tensor(out=act[:], in0=act[:], in1=gate_sb[(j, G, m)][:], op=MULT)
             if gate == O:
-                nc.vector.tensor_tensor(out=act[:], in0=act[:], in1=cell_sb[(j, m)][:], op=MULT)
+                engine = nc.gpsimd if j == 0 else nc.vector
+                engine.tensor_tensor(out=act[:], in0=act[:], in1=cell_sb[(j, m)][:], op=MULT)
                 nc.sync.dma_start(out=h1_rows[:, m, HS * j : HS * (j + 1)], in_=act[:])
 
         def cell_update(j, gate, m):

@@ -77,6 +77,7 @@ def tile_symlstmcell_kernel(
         psum = ctx.enter_context(tc.psum_pool(name="psum", bufs=4))
 
         x_raw = keep.tile([P, 2, M_TILES, WIDTH], BF16)
+        x_sorted = keep.tile([P, 2, M_TILES, WIDTH], BF16)
         x_grouped = keep.tile([P, M_TILES, PASSES, 4 * P], BF16, align_bytes=64)
         x_codes = keep.tile([P, M_TILES, PASSES, P], U32, align_bytes=64)
         x_scales = keep.tile([P, M_TILES, PASSES, P], U8, align_bytes=64)
@@ -170,16 +171,19 @@ def tile_symlstmcell_kernel(
                 )
             engine_copy(out=bias_sb[:, n, :], in_=spread[:])
 
+        def sort_x(s, m):
+            nc.vector.tensor_copy(
+                out=x_sorted[:, s, m, :].bitcast(F32).rearrange("r (g u p) -> r g u p", g=HALVES, u=2),
+                in_=x_raw[:, s, m, :].bitcast(F32).rearrange("r (g p u) -> r g u p", g=HALVES, u=2),
+            )
+
         def transpose_x(s, m, which):
-            x_words = x_raw[:, s, m, :].bitcast(F32)
+            x_words = x_sorted[:, s, m, :].bitcast(F32)
             planes = bank([P, HALVES, 2, P], which)
             for g in range(HALVES):
                 for u in range(2):
-                    nc.tensor.transpose(
-                        planes[:, g, u, :],
-                        x_words[:, 2 * P * g + u : 2 * P * (g + 1) : 2],
-                        ident[:],
-                    )
+                    first = P * (2 * g + u)
+                    nc.tensor.transpose(planes[:, g, u, :], x_words[:, first : first + P], ident[:])
             return planes
 
         def regroup_x(engine_copy, s, m, planes):
@@ -198,6 +202,8 @@ def tile_symlstmcell_kernel(
             )
 
         def prepare(s, sets):
+            for m in range(M_TILES):
+                sort_x(s, m)
             for m in range(M_TILES):
                 planes = transpose_x(s, m, sets[m % 2])
                 regroup_x(nc.scalar.copy if m % 2 == 0 else nc.vector.tensor_copy, s, m, planes)
@@ -221,7 +227,7 @@ def tile_symlstmcell_kernel(
                 )
 
         for i, n in enumerate(chunk_order[:WARM_UP]):
-            spread_bias(n, "ab"[i % 2], nc.scalar.copy if i % 2 == 0 else nc.vector.tensor_copy)
+            spread_bias(n, "ab"[i % 2], nc.scalar.copy)
         prepare(0, "ab")
         for n in chunk_order[WARM_UP:]:
             spread_bias(n, "b", nc.scalar.copy)

@@ -229,13 +229,15 @@ def tile_symlstmcell_kernel(
         for i, n in enumerate(chunk_order[:WARM_UP]):
             spread_bias(n, "ab"[i % 2], nc.scalar.copy)
         prepare(0, "ab")
-        for n in chunk_order[WARM_UP:]:
+        for n in chunk_order[WARM_UP : WARM_UP + 2]:
             spread_bias(n, "b", nc.scalar.copy)
         open_acc = {}
         for (j, gate, m) in steps[:M_TILES]:
             open_acc[m] = bank([P, HS], "a")
             passes(open_acc[m], j, gate, m, 0)
         prepare(1, "bb")
+        for n in chunk_order[WARM_UP + 2 :]:
+            spread_bias(n, "b", nc.scalar.copy)
 
         gate_sb = {}
         cell_sb = {}

@@ -29,6 +29,7 @@ CHUNKS = GROUPS * GATES
 GATE_COLS = CHUNKS * HS
 BIAS_W = 256
 BIAS_ROWS = GATE_COLS // BIAS_W
+OPEN_AHEAD = 8
 WARM_UP = 4
 PRODUCT_LAG = 2
 CELL_LAG = 3
@@ -141,20 +142,26 @@ def tile_symlstmcell_kernel(
         )
         nc.vector.memset(planes_hh[:].bitcast(I32), 0)
 
-        first_chunk = chunk_order[0]
-        for s in range(2):
-            load_x(s, 0)
-            load_x(s, 1)
-            load_weight_scales(s, 0)
-            load_weight_chunk(first_chunk, s)
-        for position, n in enumerate(chunk_order[1:]):
+        first_chunk, second_chunk = chunk_order[0], chunk_order[1]
+        load_x(0, 0)
+        load_x(0, 1)
+        load_weight_scales(0, 0)
+        load_weight_chunk(first_chunk, 0)
+        load_x(1, 0)
+        load_x(1, 1)
+        load_weight_chunk(second_chunk, 0)
+        load_weight_scales(1, 0)
+        load_weight_chunk(first_chunk, 1)
+        load_weight_chunk(second_chunk, 1)
+        load_c0(0)
+        for position, n in enumerate(chunk_order[2:]):
             if n == GATES + F:
                 for s in range(2):
                     load_weight_scales(s, 1)
             for s in range(2):
                 load_weight_chunk(n, s)
-            if position < 2:
-                load_c0(position)
+            if position == 0:
+                load_c0(1)
 
         nc.scalar.activation(out=warm[:], in_=warm[:], func=SIGMOID)
 
@@ -232,12 +239,15 @@ def tile_symlstmcell_kernel(
         for n in chunk_order[WARM_UP : WARM_UP + 2]:
             spread_bias(n, "b", nc.scalar.copy)
         open_acc = {}
-        for (j, gate, m) in steps[:M_TILES]:
-            open_acc[m] = bank([P, HS], "a")
-            passes(open_acc[m], j, gate, m, 0)
+        for q in range(M_TILES):
+            open_acc[q] = bank([P, HS], "a")
+            passes(open_acc[q], steps[q][0], steps[q][1], steps[q][2], 0)
         prepare(1, "bb")
         for n in chunk_order[WARM_UP + 2 :]:
             spread_bias(n, "b", nc.scalar.copy)
+        for q in range(M_TILES, OPEN_AHEAD):
+            open_acc[q] = bank([P, HS], "b")
+            passes(open_acc[q], steps[q][0], steps[q][1], steps[q][2], 0)
 
         gate_sb = {}
         cell_sb = {}
@@ -245,8 +255,8 @@ def tile_symlstmcell_kernel(
         def gate_block(q):
             j, gate, m = steps[q]
             n = GATES * j + gate
-            if q < M_TILES:
-                acc = open_acc[m]
+            if q < OPEN_AHEAD:
+                acc = open_acc[q]
             else:
                 acc = bank([P, HS], "ba"[q % 2])
                 passes(acc, j, gate, m, 0)

@@ -119,11 +119,11 @@ def tile_symlstmcell_kernel(
                 in_=all_words[:, :, HS * n : HS * (n + 1)],
             )
 
-        def load_c0(half):
+        def load_c0(j):
             rows = c0.rearrange("(p m) h -> p m h", m=M_TILES)
             nc.sync.dma_start(
-                out=c0_sb[:, 2 * half : 2 * half + 2, :],
-                in_=rows[:, 2 * half : 2 * half + 2, :],
+                out=c0_sb[:, :, HS * j : HS * (j + 1)],
+                in_=rows[:, :, HS * j : HS * (j + 1)],
             )
 
         nc.vector.memset(planes_ih[:].bitcast(I32), 0)
@@ -160,7 +160,7 @@ def tile_symlstmcell_kernel(
                     load_weight_scales(s, 1)
             for s in range(2):
                 load_weight_chunk(n, s)
-            if position == 0:
+            if n == GATES + I:
                 load_c0(1)
 
         nc.scalar.activation(out=warm[:], in_=warm[:], func=SIGMOID)

from contextlib import ExitStack

import concourse.mybir as mybir
from concourse.masks import make_identity

F32 = mybir.dt.float32
BF16 = mybir.dt.bfloat16
I32 = mybir.dt.int32
U32 = mybir.dt.uint32
U8 = mybir.dt.uint8
FP8X4 = mybir.dt.float8_e4m3fn_x4
ADD = mybir.AluOpType.add
MULT = mybir.AluOpType.mult
TANH = mybir.ActivationFunctionType.Tanh
SIGMOID = mybir.ActivationFunctionType.Sigmoid

P = 128
BATCH = 512
M_TILES = BATCH // P
WIDTH = 1024
K_PASS = 4 * P
HALVES = WIDTH // K_PASS
PASSES = 2 * HALVES
HS = 512
G, I, F, O = 0, 1, 2, 3
GATES = 4
GROUPS = 2
CHUNKS = GROUPS * GATES
GATE_COLS = CHUNKS * HS
BIAS_W = 256
BIAS_ROWS = GATE_COLS // BIAS_W
OPEN_AHEAD = 8
WARM_UP = 4
PRODUCT_LAG = 2
CELL_LAG = 3
LAST_LAG = 1
FIRST_C0_LAG = 4

FLOPS = 2 * BATCH * (2 * WIDTH) * GATE_COLS


def tile_symlstmcell_kernel(
    tc,
    x_in,
    h0,
    c0,
    w_ih_words,
    w_ih_scales,
    w_hh_words,
    w_hh_scales,
    bias_ih,
    bias_hh,
    h1_out,
    c1_out,
):
    nc = tc.nc
    sources = (x_in, h0)
    words = (w_ih_words, w_hh_words)
    scales = (w_ih_scales, w_hh_scales)
    h1_rows = h1_out.rearrange("(p m) h -> p m h", m=M_TILES)
    c1_rows = c1_out.rearrange("(p m) h -> p m h", m=M_TILES)

    steps = []
    for gate in (F, G, I):
        steps += [(0, gate, m) for m in range(M_TILES)]
    steps += [(1, F, m) for m in range(M_TILES)]
    for m in range(M_TILES):
        steps += [(1, G, m), (1, I, m)]
    for j in range(GROUPS):
        steps += [(j, O, m) for m in range(M_TILES)]
    chunk_order = [GATES * j + gate for (j, gate, m) in steps if m == 0]

    with ExitStack() as ctx:
        ctx.enter_context(tc.manual_schedule())
        keep = ctx.enter_context(tc.tile_pool(name="keep", bufs=1))
        work = ctx.enter_context(tc.tile_pool(name="work", bufs=M_TILES))
        late = ctx.enter_context(tc.tile_pool(name="late", bufs=GROUPS * M_TILES))
        psum = ctx.enter_context(tc.psum_pool(name="psum", bufs=4))

        x_raw = keep.tile([P, 2, M_TILES, WIDTH], BF16)
        x_sorted = keep.tile([P, 2, M_TILES, WIDTH], BF16)
        x_grouped = keep.tile([P, M_TILES, PASSES, 4 * P], BF16, align_bytes=64)
        x_codes = keep.tile([P, M_TILES, PASSES, P], U32, align_bytes=64)
        x_scales = keep.tile([P, M_TILES, PASSES, P], U8, align_bytes=64)
        w_codes = keep.tile([P, PASSES, GATE_COLS], U32, align_bytes=64)
        planes_ih = keep.tile([P, GATE_COLS], U8, align_bytes=64)
        planes_hh = keep.tile([P, GATE_COLS], U8, align_bytes=64)
        w_planes = (planes_ih, planes_hh)
        c0_sb = keep.tile([P, M_TILES, WIDTH], BF16)
        bias_rows = keep.tile([P, BIAS_W], BF16)
        bias_pick = keep.tile([P, BIAS_ROWS], BF16)
        bias_sb = keep.tile([P, CHUNKS, HS], F32)
        ident = keep.tile([P, P], F32)
        warm = keep.tile([P, 1], F32)

        def bank(shape, which):
            return psum.tile(shape, F32, tag="bank_%s" % which, name="bank_%s" % which)

        def load_x(s, half):
            rows = sources[s].rearrange("(p m) k -> p m k", m=M_TILES)
            nc.sync.dma_start(
                out=x_raw[:, s, 2 * half : 2 * half + 2, :],
                in_=rows[:, 2 * half : 2 * half + 2, :],
            )

        def load_weight_scales(s, j):
            cols = slice(GATES * HS * j, GATES * HS * (j + 1))
            for quad in range(4):
                first = 32 * quad
                nc.sync.dma_start(
                    out=w_planes[s][first : first + 4 * HALVES, cols].bitcast(I32),
                    in_=scales[s][:, 4 * quad : 4 * quad + 4, cols].bitcast(I32),
                )

        def load_weight_chunk(n, s):
            all_words = words[s].rearrange("g p n t -> p g (n t)").bitcast(I32)
            nc.sync.dma_start(
                out=w_codes[:, HALVES * s : HALVES * (s + 1), HS * n : HS * (n + 1)].bitcast(I32),
                in_=all_words[:, :, HS * n : HS * (n + 1)],
            )

        def load_c0(j):
            rows = c0.rearrange("(p m) h -> p m h", m=M_TILES)
            nc.sync.dma_start(
                out=c0_sb[:, :, HS * j : HS * (j + 1)],
                in_=rows[:, :, HS * j : HS * (j + 1)],
            )

        nc.vector.memset(planes_ih[:].bitcast(I32), 0)
        nc.sync.dma_start(
            out=bias_rows[0:BIAS_ROWS, :], in_=bias_ih.rearrange("(v c) -> v c", c=BIAS_W)
        )
        nc.sync.dma_start(
            out=bias_rows[BIAS_ROWS : 2 * BIAS_ROWS, :], in_=bias_hh.rearrange("(v c) -> v c", c=BIAS_W)
        )
        nc.vector.memset(bias_rows[32:64, :], 0.0)
        nc.vector.memset(bias_rows[64:128, :], 0.0)
        nc.vector.memset(warm[:], 0.0)
        make_identity(nc, ident[:])
        nc.vector.tensor_tensor(
            out=bias_pick[:], in0=ident[:, 0:BIAS_ROWS], in1=ident[:, BIAS_ROWS : 2 * BIAS_ROWS], op=ADD
        )
        nc.vector.memset(planes_hh[:].bitcast(I32), 0)

        first_chunk, second_chunk = chunk_order[0], chunk_order[1]
        load_x(0, 0)
        load_x(0, 1)
        load_weight_scales(0, 0)
        load_weight_chunk(first_chunk, 0)
        load_x(1, 0)
        load_x(1, 1)
        load_weight_chunk(second_chunk, 0)
        load_weight_scales(1, 0)
        load_weight_chunk(first_chunk, 1)
        load_weight_chunk(second_chunk, 1)
        load_c0(0)
        for position, n in enumerate(chunk_order[2:]):
            if n == GATES + F:
                for s in range(2):
                    load_weight_scales(s, 1)
            for s in range(2):
                load_weight_chunk(n, s)
            if n == GATES + I:
                load_c0(1)

        nc.scalar.activation(out=warm[:], in_=warm[:], func=SIGMOID)

        def spread_bias(n, which, engine_copy):
            spread = bank([P, HS], which)
            for part in range(HS // BIAS_W):
                v = (HS // BIAS_W) * n + part
                nc.tensor.matmul(
                    spread[:, BIAS_W * part : BIAS_W * (part + 1)],
                    lhsT=bias_pick[:, v : v + 1].to_broadcast([P, P]),
                    rhs=bias_rows[:],
                    start=True,
                    stop=True,
                )
            engine_copy(out=bias_sb[:, n, :], in_=spread[:])

        def sort_x(s, m):
            nc.vector.tensor_copy(
                out=x_sorted[:, s, m, :].bitcast(F32).rearrange("r (g u p) -> r g u p", g=HALVES, u=2),
                in_=x_raw[:, s, m, :].bitcast(F32).rearrange("r (g p u) -> r g u p", g=HALVES, u=2),
            )

        def transpose_x(s, m, which):
            x_words = x_sorted[:, s, m, :].bitcast(F32)
            planes = bank([P, HALVES, 2, P], which)
            for g in range(HALVES):
                for u in range(2):
                    first = P * (2 * g + u)
                    nc.tensor.transpose(planes[:, g, u, :], x_words[:, first : first + P], ident[:])
            return planes

        def regroup_x(engine_copy, s, m, planes):
            dst = x_grouped[:, m, HALVES * s : HALVES * (s + 1), :].bitcast(F32)
            engine_copy(
                out=dst.rearrange("p g (r u) -> p g r u", u=2),
                in_=planes[:].rearrange("p g u r -> p g r u"),
            )

        def quantise_x(s, m):
            both = slice(HALVES * s, HALVES * (s + 1))
            nc.vector.quantize_mx(
                out=x_codes[:, m, both, :].rearrange("p g r -> p (g r)").bitcast(FP8X4),
                scales=x_scales[:, m, both, :].rearrange("p g r -> p (g r)"),
                in_=x_grouped[:, m, both, :].rearrange("p g w -> p (g w)"),
            )

        def prepare(s, sets):
            for m in range(M_TILES):
                sort_x(s, m)
            for m in range(M_TILES):
                planes = transpose_x(s, m, sets[m % 2])
                regroup_x(nc.scalar.copy if m % 2 == 0 else nc.vector.tensor_copy, s, m, planes)
                if m >= 1:
                    quantise_x(s, m - 1)
            quantise_x(s, M_TILES - 1)

        def passes(acc, j, gate, m, s):
            n = GATES * j + gate
            cols = slice(HS * n, HS * (n + 1))
            for g in range(HALVES):
                c = HALVES * s + g
                nc.tensor.matmul_mx(
                    out=acc[:],
                    lhsT=x_codes[:, m, c, :].bitcast(FP8X4),
                    lhsT_scale=x_scales[:, m, c, :],
                    rhs=w_codes[:, c, cols].bitcast(FP8X4),
                    rhs_scale=w_planes[s][4 * g : P, cols],
                    start=(c == 0),
                    stop=(c == PASSES - 1),
                )

        for i, n in enumerate(chunk_order[:WARM_UP]):
            spread_bias(n, "ab"[i % 2], nc.scalar.copy)
        prepare(0, "ab")
        for n in chunk_order[WARM_UP : WARM_UP + 2]:
            spread_bias(n, "b", nc.scalar.copy)
        open_acc = {}
        for q in range(M_TILES):
            open_acc[q] = bank([P, HS], "a")
            passes(open_acc[q], steps[q][0], steps[q][1], steps[q][2], 0)
        prepare(1, "bb")
        for n in chunk_order[WARM_UP + 2 :]:
            spread_bias(n, "b", nc.scalar.copy)
        for q in range(M_TILES, OPEN_AHEAD):
            open_acc[q] = bank([P, HS], "b")
            passes(open_acc[q], steps[q][0], steps[q][1], steps[q][2], 0)

        gate_sb = {}
        cell_sb = {}

        def gate_block(q):
            j, gate, m = steps[q]
            n = GATES * j + gate
            if q < OPEN_AHEAD:
                acc = open_acc[q]
            else:
                acc = bank([P, HS], "ba"[q % 2])
                passes(acc, j, gate, m, 0)
            passes(acc, j, gate, m, 1)
            pool = late if gate == O else work
            act = pool.tile([P, HS], F32, tag="gate%d" % gate, name="act")
            nc.vector.tensor_tensor(out=act[:], in0=acc[:], in1=bias_sb[:, n, :], op=ADD)
            nc.scalar.activation(out=act[:], in_=act[:], func=TANH if gate == G else SIGMOID)
            gate_sb[(j, gate, m)] = act

        def gate_product(j, gate, m):
            act = gate_sb[(j, gate, m)]
            if gate == F:
                nc.gpsimd.tensor_tensor(out=act[:], in0=act[:], in1=c0_sb[:, m, HS * j : HS * (j + 1)], op=MULT)
            if gate == I:
                nc.vector.tensor_tensor(out=act[:], in0=act[:], in1=gate_sb[(j, G, m)][:], op=MULT)
            if gate == O:
                engine = nc.gpsimd if j == 0 else nc.vector
                engine.tensor_tensor(out=act[:], in0=act[:], in1=cell_sb[(j, m)][:], op=MULT)
                nc.sync.dma_start(out=h1_rows[:, m, HS * j : HS * (j + 1)], in_=act[:])

        def cell_update(j, gate, m):
            c1 = work.tile([P, HS], F32, tag="c1")
            nc.vector.tensor_tensor(
                out=c1[:], in0=gate_sb[(j, I, m)][:], in1=gate_sb[(j, F, m)][:], op=ADD
            )
            nc.sync.dma_start(out=c1_rows[:, m, HS * j : HS * (j + 1)], in_=c1[:])
            tanh_c1 = late.tile([P, HS], F32, tag="tanh_c1")
            nc.scalar.activation(out=tanh_c1[:], in_=c1[:], func=TANH)
            cell_sb[(j, m)] = tanh_c1

        updates = {}
        products = {}
        for q, (j, gate, m) in enumerate(steps):
            lag = PRODUCT_LAG
            if j == 0 and gate == F:
                lag = FIRST_C0_LAG
            if j == 1 and gate == O:
                lag = LAST_LAG
            products.setdefault(q + lag, []).append((j, gate, m))
            if gate == I:
                updates.setdefault(q + CELL_LAG, []).append((j, gate, m))
        for q in range(len(steps) + CELL_LAG):
            if q < len(steps):
                gate_block(q)
            for block in updates.get(q, []):
                cell_update(*block)
            for block in products.get(q, []):
                gate_product(*block)
